import numpy as np
import ml_dtypes


def mxq(x, axis, fmt="e4m3"):
    dtype, down = {"e4m3": (ml_dtypes.float8_e4m3fn, 7), "e5m2": (ml_dtypes.float8_e5m2, 14)}[fmt]
    v = np.moveaxis(np.asarray(x, np.float32).astype(ml_dtypes.bfloat16).astype(np.float64), axis, -1)
    blocks = v.reshape(v.shape[:-1] + (-1, 32))
    amax = np.abs(blocks).max(-1, keepdims=True)
    byte = np.maximum(np.where(amax > 0, np.frexp(amax)[1] - 1 + 127, 0) - down, 1)
    scale = np.exp2(byte - 127.0)
    codes = (blocks / scale).astype(np.float32).astype(dtype).astype(np.float64)
    return np.moveaxis((codes * scale).reshape(v.shape), -1, axis)


WIDE = False


def mx_kscale(k):
    if not WIDE:
        return np.ones(k)
    levels = np.array([10, -10, 5, -5, 0])
    a = np.random.permutation(np.resize(levels, k // 512 * 4)).reshape(k // 512, 4)
    idx = np.arange(k)
    return np.exp2(a[idx // 512, idx % 128 // 32])


BF16 = ml_dtypes.bfloat16


def bf(x):
    return np.asarray(x, np.float32).astype(BF16)


def f64(x):
    return np.asarray(x).astype(np.float64)


E2M1 = np.array([0.0, 0.5, 1.0, 1.5, 2.0, 3.0, 4.0, 6.0, -0.0, -0.5, -1.0, -1.5, -2.0, -3.0, -4.0, -6.0])


def pack_weight(w, fmt):
    k, n = w.shape
    w = f64(bf(w)).reshape(k // 32, 32, n)
    amax = np.abs(w).max(1)
    if fmt == "e4m3":
        byte = np.frexp(amax)[1] - 1 + 127 - 7
    else:
        mant, ex = np.frexp(amax / 6.0)
        byte = np.where(mant > 0.5, ex, ex - 1) + 127
    byte = np.clip(np.where(amax > 0, byte, 1), 1, 254)
    scaled = (w * np.exp2(127.0 - byte)[:, None, :]).reshape(k, n).astype(np.float32)
    by_word = np.ascontiguousarray(scaled.reshape(k // 512, 128, 4, n).transpose(0, 1, 3, 2))
    if fmt == "e4m3":
        words = by_word.astype(ml_dtypes.float8_e4m3fn).view(np.uint8)
    else:
        c = by_word.astype(ml_dtypes.float4_e2m1fn).view(np.uint8) & 0xF
        words = c[..., 0::2] | (c[..., 1::2] << 4)
    return np.ascontiguousarray(words), np.ascontiguousarray(byte.astype(np.uint8).reshape(k // 512, 16, n))


def unpack_weight(words, scales, fmt):
    g, p, n, _ = words.shape
    if fmt == "e4m3":
        vals = np.ascontiguousarray(words).view(ml_dtypes.float8_e4m3fn).astype(np.float64)
    else:
        nib = np.empty((g, p, n, 4), np.uint8)
        nib[..., 0::2] = words & 0xF
        nib[..., 1::2] = words >> 4
        vals = E2M1[nib]
    vals = vals * np.repeat(np.exp2(scales.astype(np.float64) - 127.0), 8, axis=1)[..., None]
    return vals.transpose(0, 1, 3, 2).reshape(g * 512, n)


B, SIDE, HE, Z, HD, XO = 1024, 32, 1024, 512, 2048, 1024
FMT = "e4m3"


def setup_inputs():
    n = np.random.standard_normal
    s = mx_kscale(HD)
    hd = bf(np.tanh(n((B, HD))) * s)
    w_mu = n((XO, HD)) * 1.5 / np.sqrt(HD) / s[None, :]
    mu_words, mu_scales = pack_weight(np.ascontiguousarray(w_mu.T), FMT)
    b_mu_d = bf(n(XO) * 0.3)
    w_ls = n((XO, HD)) * 1.5 / np.sqrt(HD) / s[None, :]
    ls_words, ls_scales = pack_weight(np.ascontiguousarray(w_ls.T), FMT)
    b_ls_d = bf(n(XO) * 0.3)
    eps_x = bf(n((B, XO)))
    return {"hd": hd,
            "W_mu_d_words": mu_words,
            "W_mu_d_scales": mu_scales,
            "b_mu_d": b_mu_d,
            "W_ls_d_words": ls_words,
            "W_ls_d_scales": ls_scales,
            "b_ls_d": b_ls_d,
            "eps_x": eps_x}


def reference(hd, W_mu_d_words, W_mu_d_scales, b_mu_d, W_ls_d_words, W_ls_d_scales, b_ls_d, eps_x):
    hq = mxq(f64(hd), 1, "e4m3")
    mu_d = (hq @ unpack_weight(W_mu_d_words, W_mu_d_scales, FMT)) + f64(b_mu_d)
    ls_d = (hq @ unpack_weight(W_ls_d_words, W_ls_d_scales, FMT)) + f64(b_ls_d)
    return mu_d + np.exp(0.5 * ls_d) * f64(eps_x)

@@ -1,0 +1,189 @@
+from contextlib import ExitStack
+
+import concourse.mybir as mybir
+from concourse.masks import make_identity
+
+F32 = mybir.dt.float32
+BF16 = mybir.dt.bfloat16
+U8 = mybir.dt.uint8
+U32 = mybir.dt.uint32
+I32 = mybir.dt.int32
+FP8X4 = mybir.dt.float8_e4m3fn_x4
+ADD = mybir.AluOpType.add
+MULT = mybir.AluOpType.mult
+EXP = mybir.ActivationFunctionType.Exp
+
+P = 128
+PACK = 4
+K_PASS = P * PACK
+ROWS = 1024
+K = 2048
+N = 1024
+N_CHUNK = 512
+ROW_TILES = ROWS // P
+PASSES = K // K_PASS
+HALVES = N // N_CHUNK
+QUADRANTS = 4
+AHEAD = 2
+MU = "mu"
+LS = "ls"
+
+FLOPS = 2 * ROWS * K * 2 * N
+
+
+def tile_vae_pb_kernel(
+    tc, hd, w_mu_words, w_mu_scales, b_mu, w_ls_words, w_ls_scales, b_ls, eps_x, out
+):
+    nc = tc.nc
+    words_dram = {MU: w_mu_words, LS: w_ls_words}
+    scales_dram = {MU: w_mu_scales, LS: w_ls_scales}
+    bias_dram = {MU: b_mu, LS: b_ls}
+
+    with ExitStack() as ctx:
+        keep = ctx.enter_context(tc.tile_pool(name="keep", bufs=1))
+        stage = ctx.enter_context(tc.tile_pool(name="stage", bufs=3))
+        work = ctx.enter_context(tc.tile_pool(name="work", bufs=4))
+        results = ctx.enter_context(tc.tile_pool(name="results", bufs=8))
+        psum_t = ctx.enter_context(tc.psum_pool(name="psum_t", bufs=2))
+        psum_mx = ctx.enter_context(tc.psum_pool(name="psum_mx", bufs=6))
+
+        ident = keep.tile([P, P], F32)
+        make_identity(nc, ident[:])
+        ones = keep.tile([P, P], BF16)
+        nc.vector.memset(ones[:], 1.0)
+
+        w_planes = {}
+        for w in (LS, MU):
+            w_planes[w] = keep.tile([P, N], U8, name="planes_" + w, align_bytes=64)
+            nc.vector.memset(w_planes[w][:].bitcast(I32), 0)
+
+        bias_rows = {}
+        for w in (LS, MU):
+            bias_rows[w] = keep.tile([P, N], BF16, name="bias_rows_" + w)
+            nc.vector.memset(bias_rows[w][:], 0.0)
+            nc.scalar.dma_start(out=bias_rows[w][0:1, :], in_=bias_dram[w].unsqueeze(0))
+
+        hd_sb = [keep.tile([P, K], BF16, name="hd%d" % m) for m in range(ROW_TILES)]
+        eps_sb = [keep.tile([P, N], BF16, name="eps%d" % m) for m in range(ROW_TILES)]
+        w_words = {}
+
+        def load_hd(m):
+            nc.sync.dma_start(out=hd_sb[m][:], in_=hd[m * P : (m + 1) * P, :])
+
+        def load_eps(m):
+            nc.sync.dma_start(out=eps_sb[m][:], in_=eps_x[m * P : (m + 1) * P, :])
+
+        def load_scales(w):
+            for quad in range(QUADRANTS):
+                nc.sync.dma_start(
+                    out=w_planes[w][32 * quad : 32 * quad + 16, :].bitcast(I32),
+                    in_=scales_dram[w][:, 4 * quad : 4 * quad + 4, :].bitcast(I32),
+                )
+
+        def load_words(w, h):
+            for g in range(PASSES):
+                w_words[(w, h, g)] = keep.tile(
+                    [P, N_CHUNK], U32, name="words_%s_%d_%d" % (w, h, g), align_bytes=64
+                )
+                byte_cols = slice(h * N_CHUNK * PACK, (h + 1) * N_CHUNK * PACK)
+                nc.sync.dma_start(
+                    out=w_words[(w, h, g)][:].bitcast(I32),
+                    in_=words_dram[w][g].rearrange("p n t -> p (n t)")[:, byte_cols].bitcast(I32),
+                )
+
+        load_hd(0)
+        load_hd(1)
+        load_scales(LS)
+        load_words(LS, 0)
+        load_hd(2)
+        load_scales(MU)
+        load_words(MU, 0)
+        load_eps(0)
+        for m in range(3, ROW_TILES):
+            load_hd(m)
+            load_eps(m - 2)
+        load_eps(ROW_TILES - 2)
+        load_eps(ROW_TILES - 1)
+        load_words(LS, 1)
+        load_words(MU, 1)
+
+        hd_codes = [
+            keep.tile([P, PASSES * P], U32, name="hd_codes%d" % m, align_bytes=64)
+            for m in range(ROW_TILES)
+        ]
+        hd_scales = [
+            keep.tile([P, PASSES * P], U8, name="hd_scales%d" % m, align_bytes=64)
+            for m in range(ROW_TILES)
+        ]
+
+        def transpose_and_quantise(m):
+            pairs = hd_sb[m][:].bitcast(F32)
+            grouped = stage.tile([P, PASSES, P, PACK], BF16, align_bytes=64)
+            for first in range(0, PASSES, 2):
+                flipped = psum_t.tile([P, 2, 2, P], F32)
+                for j in range(2):
+                    g = first + j
+                    for u in range(2):
+                        nc.tensor.transpose(
+                            flipped[:, j, u, :],
+                            pairs[:, 256 * g + u : 256 * (g + 1) : 2],
+                            ident[:],
+                        )
+                nc.scalar.copy(
+                    out=grouped[:, first : first + 2, :, :].bitcast(F32),
+                    in_=flipped[:].rearrange("p g u r -> p g r u"),
+                )
+            nc.vector.quantize_mx(
+                out=hd_codes[m][:].bitcast(FP8X4),
+                scales=hd_scales[m][:],
+                in_=grouped[:].rearrange("p g r t -> p (g r t)"),
+            )
+
+        bias_all = {}
+
+        def broadcast_bias(w):
+            bias_all[w] = keep.tile([P, N], F32, name="bias_all_" + w)
+            for h in range(HALVES):
+                cols = slice(h * N_CHUNK, (h + 1) * N_CHUNK)
+                acc = psum_mx.tile([P, N_CHUNK], F32)
+                nc.tensor.matmul(acc[:], lhsT=ones[:], rhs=bias_rows[w][:, cols], start=True, stop=True)
+                nc.scalar.copy(out=bias_all[w][:, cols], in_=acc[:])
+
+        def mx_group(m, w, h):
+            cols = slice(h * N_CHUNK, (h + 1) * N_CHUNK)
+            acc = psum_mx.tile([P, N_CHUNK], F32)
+            for g in range(PASSES):
+                rows = slice(g * P, (g + 1) * P)
+                nc.tensor.matmul_mx(
+                    out=acc[:],
+                    lhsT=hd_codes[m][:, rows].bitcast(FP8X4),
+                    lhsT_scale=hd_scales[m][:, rows],
+                    rhs=w_words[(w, h, g)][:].bitcast(FP8X4),
+                    rhs_scale=w_planes[w][4 * g : P, cols],
+                    start=(g == 0),
+                    stop=(g == PASSES - 1),
+                )
+            return acc
+
+        transpose_and_quantise(0)
+        broadcast_bias(LS)
+        broadcast_bias(MU)
+        transpose_and_quantise(1)
+
+        for h in range(HALVES):
+            cols = slice(h * N_CHUNK, (h + 1) * N_CHUNK)
+            for m in range(ROW_TILES):
+                ls_acc = mx_group(m, LS, h)
+                noise = work.tile([P, N_CHUNK], F32)
+                nc.vector.tensor_tensor(out=noise[:], in0=ls_acc[:], in1=bias_all[LS][:, cols], op=ADD)
+                nc.scalar.activation(out=noise[:], in_=noise[:], func=EXP, scale=0.5)
+                nc.vector.tensor_tensor(out=noise[:], in0=noise[:], in1=eps_sb[m][:, cols], op=MULT)
+                nc.gpsimd.tensor_tensor(out=noise[:], in0=noise[:], in1=bias_all[MU][:, cols], op=ADD)
+
+                if h == 0 and m + AHEAD < ROW_TILES:
+                    transpose_and_quantise(m + AHEAD)
+
+                mu_acc = mx_group(m, MU, h)
+                result = results.tile([P, N_CHUNK], F32)
+                nc.vector.tensor_tensor(out=result[:], in0=mu_acc[:], in1=noise[:], op=ADD)
+                nc.sync.dma_start(out=out[m * P : (m + 1) * P, cols], in_=result[:])

@@ -40,6 +40,7 @@ def tile_vae_pb_kernel(
     bias_dram = {MU: b_mu, LS: b_ls}
 
     with ExitStack() as ctx:
+        ctx.enter_context(tc.manual_schedule())
         keep = ctx.enter_context(tc.tile_pool(name="keep", bufs=1))
         stage = ctx.enter_context(tc.tile_pool(name="stage", bufs=3))
         work = ctx.enter_context(tc.tile_pool(name="work", bufs=4))
@@ -116,9 +117,12 @@ def tile_vae_pb_kernel(
             for m in range(ROW_TILES)
         ]
 
-        def transpose_and_quantise(m):
+        grouped_of = {}
+
+        def transpose(m):
             pairs = hd_sb[m][:].bitcast(F32)
             grouped = stage.tile([P, PASSES, P, PACK], BF16, align_bytes=64)
+            grouped_of[m] = grouped
             for first in range(0, PASSES, 2):
                 flipped = psum_t.tile([P, 2, 2, P], F32)
                 for j in range(2):
@@ -133,10 +137,12 @@ def tile_vae_pb_kernel(
                     out=grouped[:, first : first + 2, :, :].bitcast(F32),
                     in_=flipped[:].rearrange("p g u r -> p g r u"),
                 )
+
+        def quantise(m):
             nc.vector.quantize_mx(
                 out=hd_codes[m][:].bitcast(FP8X4),
                 scales=hd_scales[m][:],
-                in_=grouped[:].rearrange("p g r t -> p (g r t)"),
+                in_=grouped_of[m][:].rearrange("p g r t -> p (g r t)"),
             )
 
         bias_all = {}
@@ -165,25 +171,47 @@ def tile_vae_pb_kernel(
                 )
             return acc
 
-        transpose_and_quantise(0)
+        chunks = [(h, m) for h in range(HALVES) for m in range(ROW_TILES)]
+        noise_of = {}
+        mean_of = {}
+
+        def finish(c):
+            h, m = chunks[c]
+            cols = slice(h * N_CHUNK, (h + 1) * N_CHUNK)
+            noise = noise_of[c]
+            mean = mean_of[c]
+            nc.vector.tensor_tensor(out=noise[:], in0=noise[:], in1=eps_sb[m][:, cols], op=MULT)
+            adder = nc.gpsimd if c % 2 == 0 else nc.vector
+            adder.tensor_tensor(out=mean[:], in0=mean[:], in1=noise[:], op=ADD)
+            nc.sync.dma_start(out=out[m * P : (m + 1) * P, cols], in_=mean[:])
+
+        transpose(0)
         broadcast_bias(LS)
         broadcast_bias(MU)
-        transpose_and_quantise(1)
+        transpose(1)
+        quantise(0)
+        quantise(1)
 
-        for h in range(HALVES):
+        for c in range(len(chunks)):
+            h, m = chunks[c]
             cols = slice(h * N_CHUNK, (h + 1) * N_CHUNK)
-            for m in range(ROW_TILES):
-                ls_acc = mx_group(m, LS, h)
-                noise = work.tile([P, N_CHUNK], F32)
-                nc.vector.tensor_tensor(out=noise[:], in0=ls_acc[:], in1=bias_all[LS][:, cols], op=ADD)
-                nc.scalar.activation(out=noise[:], in_=noise[:], func=EXP, scale=0.5)
-                nc.vector.tensor_tensor(out=noise[:], in0=noise[:], in1=eps_sb[m][:, cols], op=MULT)
-                nc.gpsimd.tensor_tensor(out=noise[:], in0=noise[:], in1=bias_all[MU][:, cols], op=ADD)
+            prepare = h == 0 and m + AHEAD < ROW_TILES
 
-                if h == 0 and m + AHEAD < ROW_TILES:
-                    transpose_and_quantise(m + AHEAD)
+            ls_acc = mx_group(m, LS, h)
+            noise = work.tile([P, N_CHUNK], F32)
+            noise_of[c] = noise
+            nc.vector.tensor_tensor(out=noise[:], in0=ls_acc[:], in1=bias_all[LS][:, cols], op=ADD)
+            if prepare:
+                transpose(m + AHEAD)
+            nc.scalar.activation(out=noise[:], in_=noise[:], func=EXP, scale=0.5)
+            if c > 0:
+                finish(c - 1)
 
-                mu_acc = mx_group(m, MU, h)
-                result = results.tile([P, N_CHUNK], F32)
-                nc.vector.tensor_tensor(out=result[:], in0=mu_acc[:], in1=noise[:], op=ADD)
-                nc.sync.dma_start(out=out[m * P : (m + 1) * P, cols], in_=result[:])
+            mu_acc = mx_group(m, MU, h)
+            if prepare:
+                quantise(m + AHEAD)
+            mean = results.tile([P, N_CHUNK], F32)
+            mean_of[c] = mean
+            nc.vector.tensor_tensor(out=mean[:], in0=mu_acc[:], in1=bias_all[MU][:, cols], op=ADD)
+
+        finish(len(chunks) - 1)

@@ -23,8 +23,11 @@ N_CHUNK = 512
 ROW_TILES = ROWS // P
 PASSES = K // K_PASS
 HALVES = N // N_CHUNK
+CHUNKS = HALVES * ROW_TILES
 QUADRANTS = 4
-AHEAD = 2
+LEAD = 3
+TILE_LEAD = LEAD + 2
+FIRST_TILES = 2
 MU = "mu"
 LS = "ls"
 
@@ -43,26 +46,35 @@ def tile_vae_pb_kernel(
         ctx.enter_context(tc.manual_schedule())
         keep = ctx.enter_context(tc.tile_pool(name="keep", bufs=1))
         stage = ctx.enter_context(tc.tile_pool(name="stage", bufs=3))
-        work = ctx.enter_context(tc.tile_pool(name="work", bufs=4))
+        work = ctx.enter_context(tc.tile_pool(name="work", bufs=LEAD + 2))
         results = ctx.enter_context(tc.tile_pool(name="results", bufs=8))
         psum_t = ctx.enter_context(tc.psum_pool(name="psum_t", bufs=2))
         psum_mx = ctx.enter_context(tc.psum_pool(name="psum_mx", bufs=6))
 
-        ident = keep.tile([P, P], F32)
-        make_identity(nc, ident[:])
+        bias_in = {}
+        for w in (LS, MU):
+            bias_in[w] = keep.tile([1, N], BF16, name="bias_in_" + w)
+            nc.sync.dma_start(out=bias_in[w][:], in_=bias_dram[w].unsqueeze(0))
+        bias_rows = {}
+        for w in (LS, MU):
+            bias_rows[w] = keep.tile([P, N], BF16, name="bias_rows_" + w)
+            nc.vector.memset(bias_rows[w][:], 0.0)
         ones = keep.tile([P, P], BF16)
         nc.vector.memset(ones[:], 1.0)
+        ident = keep.tile([P, P], F32)
+        make_identity(nc, ident[:])
 
         w_planes = {}
         for w in (LS, MU):
             w_planes[w] = keep.tile([P, N], U8, name="planes_" + w, align_bytes=64)
             nc.vector.memset(w_planes[w][:].bitcast(I32), 0)
 
-        bias_rows = {}
+        table_warmer = keep.tile([P, 1], F32)
+        nc.vector.memset(table_warmer[:], 0.0)
+        nc.scalar.activation(out=table_warmer[:], in_=table_warmer[:], func=EXP)
+
         for w in (LS, MU):
-            bias_rows[w] = keep.tile([P, N], BF16, name="bias_rows_" + w)
-            nc.vector.memset(bias_rows[w][:], 0.0)
-            nc.scalar.dma_start(out=bias_rows[w][0:1, :], in_=bias_dram[w].unsqueeze(0))
+            nc.vector.tensor_copy(out=bias_rows[w][0:1, :], in_=bias_in[w][:])
 
         hd_sb = [keep.tile([P, K], BF16, name="hd%d" % m) for m in range(ROW_TILES)]
         eps_sb = [keep.tile([P, N], BF16, name="eps%d" % m) for m in range(ROW_TILES)]
@@ -92,21 +104,22 @@ def tile_vae_pb_kernel(
                     in_=words_dram[w][g].rearrange("p n t -> p (n t)")[:, byte_cols].bitcast(I32),
                 )
 
-        load_hd(0)
-        load_hd(1)
-        load_scales(LS)
-        load_words(LS, 0)
-        load_hd(2)
-        load_scales(MU)
-        load_words(MU, 0)
-        load_eps(0)
-        for m in range(3, ROW_TILES):
+        def load_weight_half(w, h):
+            if h == 0:
+                load_scales(w)
+            load_words(w, h)
+
+        for m in range(FIRST_TILES):
             load_hd(m)
-            load_eps(m - 2)
-        load_eps(ROW_TILES - 2)
-        load_eps(ROW_TILES - 1)
-        load_words(LS, 1)
-        load_words(MU, 1)
+        for c in range(-LEAD, CHUNKS):
+            if c + LEAD < CHUNKS and (c + LEAD) % ROW_TILES == 0:
+                load_weight_half(LS, (c + LEAD) // ROW_TILES)
+            if FIRST_TILES <= c + TILE_LEAD < ROW_TILES:
+                load_hd(c + TILE_LEAD)
+            if 0 <= c + LEAD - 1 < ROW_TILES:
+                load_eps(c + LEAD - 1)
+            if c >= 0 and c % ROW_TILES == 0:
+                load_weight_half(MU, c // ROW_TILES)
 
         hd_codes = [
             keep.tile([P, PASSES * P], U32, name="hd_codes%d" % m, align_bytes=64)
@@ -116,7 +129,6 @@ def tile_vae_pb_kernel(
             keep.tile([P, PASSES * P], U8, name="hd_scales%d" % m, align_bytes=64)
             for m in range(ROW_TILES)
         ]
-
         grouped_of = {}
 
         def transpose(m):
@@ -153,10 +165,14 @@ def tile_vae_pb_kernel(
                 cols = slice(h * N_CHUNK, (h + 1) * N_CHUNK)
                 acc = psum_mx.tile([P, N_CHUNK], F32)
                 nc.tensor.matmul(acc[:], lhsT=ones[:], rhs=bias_rows[w][:, cols], start=True, stop=True)
-                nc.scalar.copy(out=bias_all[w][:, cols], in_=acc[:])
+                nc.vector.tensor_copy(out=bias_all[w][:, cols], in_=acc[:])
 
-        def mx_group(m, w, h):
-            cols = slice(h * N_CHUNK, (h + 1) * N_CHUNK)
+        def place(c):
+            h, m = divmod(c, ROW_TILES)
+            return m, h, slice(h * N_CHUNK, (h + 1) * N_CHUNK)
+
+        def mx_group(w, c):
+            m, h, cols = place(c)
             acc = psum_mx.tile([P, N_CHUNK], F32)
             for g in range(PASSES):
                 rows = slice(g * P, (g + 1) * P)
@@ -171,47 +187,56 @@ def tile_vae_pb_kernel(
                 )
             return acc
 
-        chunks = [(h, m) for h in range(HALVES) for m in range(ROW_TILES)]
         noise_of = {}
-        mean_of = {}
 
-        def finish(c):
-            h, m = chunks[c]
-            cols = slice(h * N_CHUNK, (h + 1) * N_CHUNK)
-            noise = noise_of[c]
-            mean = mean_of[c]
-            nc.vector.tensor_tensor(out=noise[:], in0=noise[:], in1=eps_sb[m][:, cols], op=MULT)
+        def start_noise(c, ls_acc):
+            m, h, cols = place(c)
+            noise_of[c] = work.tile([P, N_CHUNK], F32, name="noise")
+            nc.vector.tensor_tensor(out=noise_of[c][:], in0=ls_acc[:], in1=bias_all[LS][:, cols], op=ADD)
+            nc.scalar.activation(out=noise_of[c][:], in_=noise_of[c][:], func=EXP, scale=0.5)
+
+        def times_eps(c):
+            m, h, cols = place(c)
+            nc.vector.tensor_tensor(out=noise_of[c][:], in0=noise_of[c][:], in1=eps_sb[m][:, cols], op=MULT)
+
+        def plus_b_mu(c):
+            m, h, cols = place(c)
             adder = nc.gpsimd if c % 2 == 0 else nc.vector
-            adder.tensor_tensor(out=mean[:], in0=mean[:], in1=noise[:], op=ADD)
-            nc.sync.dma_start(out=out[m * P : (m + 1) * P, cols], in_=mean[:])
+            adder.tensor_tensor(out=noise_of[c][:], in0=noise_of[c][:], in1=bias_all[MU][:, cols], op=ADD)
 
-        transpose(0)
+        def finish(c, mu_acc):
+            m, h, cols = place(c)
+            result = results.tile([P, N_CHUNK], F32)
+            nc.vector.tensor_tensor(out=result[:], in0=mu_acc[:], in1=noise_of[c][:], op=ADD)
+            nc.sync.dma_start(out=out[m * P : (m + 1) * P, cols], in_=result[:])
+
         broadcast_bias(LS)
         broadcast_bias(MU)
-        transpose(1)
-        quantise(0)
-        quantise(1)
+        for m in range(FIRST_TILES):
+            transpose(m)
+        for m in range(FIRST_TILES):
+            quantise(m)
 
-        for c in range(len(chunks)):
-            h, m = chunks[c]
-            cols = slice(h * N_CHUNK, (h + 1) * N_CHUNK)
-            prepare = h == 0 and m + AHEAD < ROW_TILES
+        for c in range(-LEAD, CHUNKS):
+            begins = c + LEAD < CHUNKS
+            prepares = FIRST_TILES <= c + TILE_LEAD < ROW_TILES
+            continues = 0 <= c + LEAD - 1 < CHUNKS
+            ends = c >= 0
 
-            ls_acc = mx_group(m, LS, h)
-            noise = work.tile([P, N_CHUNK], F32)
-            noise_of[c] = noise
-            nc.vector.tensor_tensor(out=noise[:], in0=ls_acc[:], in1=bias_all[LS][:, cols], op=ADD)
-            if prepare:
-                transpose(m + AHEAD)
-            nc.scalar.activation(out=noise[:], in_=noise[:], func=EXP, scale=0.5)
-            if c > 0:
-                finish(c - 1)
+            if begins:
+                ls_acc = mx_group(LS, c + LEAD)
+            if prepares:
+                transpose(c + TILE_LEAD)
+            if ends:
+                mu_acc = mx_group(MU, c)
 
-            mu_acc = mx_group(m, MU, h)
-            if prepare:
-                quantise(m + AHEAD)
-            mean = results.tile([P, N_CHUNK], F32)
-            mean_of[c] = mean
-            nc.vector.tensor_tensor(out=mean[:], in0=mu_acc[:], in1=bias_all[MU][:, cols], op=ADD)
-
-        finish(len(chunks) - 1)
+            if continues:
+                times_eps(c + LEAD - 1)
+            if begins:
+                start_noise(c + LEAD, ls_acc)
+            if continues:
+                plus_b_mu(c + LEAD - 1)
+            if prepares:
+                quantise(c + TILE_LEAD)
+            if ends:
+                finish(c, mu_acc)

@@ -26,8 +26,8 @@ HALVES = N // N_CHUNK
 CHUNKS = HALVES * ROW_TILES
 QUADRANTS = 4
 LEAD = 3
-TILE_LEAD = LEAD + 2
-FIRST_TILES = 2
+TILE_LEAD = LEAD + 3
+FIRST_TILES = 4
 MU = "mu"
 LS = "ls"
 
@@ -45,11 +45,10 @@ def tile_vae_pb_kernel(
     with ExitStack() as ctx:
         ctx.enter_context(tc.manual_schedule())
         keep = ctx.enter_context(tc.tile_pool(name="keep", bufs=1))
-        stage = ctx.enter_context(tc.tile_pool(name="stage", bufs=3))
+        stage = ctx.enter_context(tc.tile_pool(name="stage", bufs=FIRST_TILES))
         work = ctx.enter_context(tc.tile_pool(name="work", bufs=LEAD + 2))
         results = ctx.enter_context(tc.tile_pool(name="results", bufs=8))
-        psum_t = ctx.enter_context(tc.psum_pool(name="psum_t", bufs=2))
-        psum_mx = ctx.enter_context(tc.psum_pool(name="psum_mx", bufs=6))
+        psum = ctx.enter_context(tc.psum_pool(name="psum", bufs=8))
 
         bias_in = {}
         for w in (LS, MU):
@@ -94,15 +93,17 @@ def tile_vae_pb_kernel(
                 )
 
         def load_words(w, h):
-            for g in range(PASSES):
-                w_words[(w, h, g)] = keep.tile(
-                    [P, N_CHUNK], U32, name="words_%s_%d_%d" % (w, h, g), align_bytes=64
-                )
-                byte_cols = slice(h * N_CHUNK * PACK, (h + 1) * N_CHUNK * PACK)
+            byte_cols = slice(h * N_CHUNK * PACK, (h + 1) * N_CHUNK * PACK)
+            for first in range(0, PASSES, 2):
+                pair = keep.tile([P, 2, N_CHUNK], U32, name="words_%s_%d_%d" % (w, h, first), align_bytes=64)
                 nc.sync.dma_start(
-                    out=w_words[(w, h, g)][:].bitcast(I32),
-                    in_=words_dram[w][g].rearrange("p n t -> p (n t)")[:, byte_cols].bitcast(I32),
+                    out=pair[:].bitcast(I32),
+                    in_=words_dram[w][first : first + 2]
+                    .rearrange("g p n t -> p g (n t)")[:, :, byte_cols]
+                    .bitcast(I32),
                 )
+                for j in range(2):
+                    w_words[(w, h, first + j)] = pair[:, j, :]
 
         def load_weight_half(w, h):
             if h == 0:
@@ -136,7 +137,7 @@ def tile_vae_pb_kernel(
             grouped = stage.tile([P, PASSES, P, PACK], BF16, align_bytes=64)
             grouped_of[m] = grouped
             for first in range(0, PASSES, 2):
-                flipped = psum_t.tile([P, 2, 2, P], F32)
+                flipped = psum.tile([P, 2, 2, P], F32, name="bank")
                 for j in range(2):
                     g = first + j
                     for u in range(2):
@@ -163,7 +164,7 @@ def tile_vae_pb_kernel(
             bias_all[w] = keep.tile([P, N], F32, name="bias_all_" + w)
             for h in range(HALVES):
                 cols = slice(h * N_CHUNK, (h + 1) * N_CHUNK)
-                acc = psum_mx.tile([P, N_CHUNK], F32)
+                acc = psum.tile([P, N_CHUNK], F32, name="bank")
                 nc.tensor.matmul(acc[:], lhsT=ones[:], rhs=bias_rows[w][:, cols], start=True, stop=True)
                 nc.vector.tensor_copy(out=bias_all[w][:, cols], in_=acc[:])
 
@@ -171,17 +172,17 @@ def tile_vae_pb_kernel(
             h, m = divmod(c, ROW_TILES)
             return m, h, slice(h * N_CHUNK, (h + 1) * N_CHUNK)
 
-        def mx_group(w, c):
+        def mx_group(w, c, first=0, width=N_CHUNK):
             m, h, cols = place(c)
-            acc = psum_mx.tile([P, N_CHUNK], F32)
+            acc = psum.tile([P, width], F32, name="bank")
             for g in range(PASSES):
                 rows = slice(g * P, (g + 1) * P)
                 nc.tensor.matmul_mx(
                     out=acc[:],
                     lhsT=hd_codes[m][:, rows].bitcast(FP8X4),
                     lhsT_scale=hd_scales[m][:, rows],
-                    rhs=w_words[(w, h, g)][:].bitcast(FP8X4),
-                    rhs_scale=w_planes[w][4 * g : P, cols],
+                    rhs=w_words[(w, h, g)][:, first : first + width].bitcast(FP8X4),
+                    rhs_scale=w_planes[w][4 * g : P, cols.start + first : cols.start + first + width],
                     start=(g == 0),
                     stop=(g == PASSES - 1),
                 )
@@ -204,11 +205,15 @@ def tile_vae_pb_kernel(
             adder = nc.gpsimd if c % 2 == 0 else nc.vector
             adder.tensor_tensor(out=noise_of[c][:], in0=noise_of[c][:], in1=bias_all[MU][:, cols], op=ADD)
 
-        def finish(c, mu_acc):
+        def finish(c, mu_acc, first=0, width=N_CHUNK):
             m, h, cols = place(c)
-            result = results.tile([P, N_CHUNK], F32)
-            nc.vector.tensor_tensor(out=result[:], in0=mu_acc[:], in1=noise_of[c][:], op=ADD)
-            nc.sync.dma_start(out=out[m * P : (m + 1) * P, cols], in_=result[:])
+            result = results.tile([P, width], F32, name="result")
+            nc.vector.tensor_tensor(
+                out=result[:], in0=mu_acc[:], in1=noise_of[c][:, first : first + width], op=ADD
+            )
+            nc.sync.dma_start(
+                out=out[m * P : (m + 1) * P, cols.start + first : cols.start + first + width], in_=result[:]
+            )
 
         broadcast_bias(LS)
         broadcast_bias(MU)
@@ -227,8 +232,9 @@ def tile_vae_pb_kernel(
                 ls_acc = mx_group(LS, c + LEAD)
             if prepares:
                 transpose(c + TILE_LEAD)
+            parts = [(0, N_CHUNK)] if c < CHUNKS - 1 else [(0, N_CHUNK // 2), (N_CHUNK // 2, N_CHUNK // 2)]
             if ends:
-                mu_acc = mx_group(MU, c)
+                mu_accs = [mx_group(MU, c, first, width) for first, width in parts]
 
             if continues:
                 times_eps(c + LEAD - 1)
@@ -239,4 +245,5 @@ def tile_vae_pb_kernel(
             if prepares:
                 quantise(c + TILE_LEAD)
             if ends:
-                finish(c, mu_acc)
+                for mu_acc, (first, width) in zip(mu_accs, parts):
+                    finish(c, mu_acc, first, width)

@@ -25,7 +25,8 @@ PASSES = K // K_PASS
 HALVES = N // N_CHUNK
 CHUNKS = HALVES * ROW_TILES
 QUADRANTS = 4
-LEAD = 3
+LEAD = 5
+NOISE_LAG = 2
 TILE_LEAD = LEAD + 3
 FIRST_TILES = 4
 MU = "mu"
@@ -46,7 +47,7 @@ def tile_vae_pb_kernel(
         ctx.enter_context(tc.manual_schedule())
         keep = ctx.enter_context(tc.tile_pool(name="keep", bufs=1))
         stage = ctx.enter_context(tc.tile_pool(name="stage", bufs=FIRST_TILES))
-        work = ctx.enter_context(tc.tile_pool(name="work", bufs=LEAD + 2))
+        work = ctx.enter_context(tc.tile_pool(name="work", bufs=LEAD + 3))
         results = ctx.enter_context(tc.tile_pool(name="results", bufs=8))
         psum = ctx.enter_context(tc.psum_pool(name="psum", bufs=8))
 
@@ -117,8 +118,8 @@ def tile_vae_pb_kernel(
                 load_weight_half(LS, (c + LEAD) // ROW_TILES)
             if FIRST_TILES <= c + TILE_LEAD < ROW_TILES:
                 load_hd(c + TILE_LEAD)
-            if 0 <= c + LEAD - 1 < ROW_TILES:
-                load_eps(c + LEAD - 1)
+            if 0 <= c + LEAD - NOISE_LAG < ROW_TILES:
+                load_eps(c + LEAD - NOISE_LAG)
             if c >= 0 and c % ROW_TILES == 0:
                 load_weight_half(MU, c // ROW_TILES)
 
@@ -202,8 +203,7 @@ def tile_vae_pb_kernel(
 
         def plus_b_mu(c):
             m, h, cols = place(c)
-            adder = nc.gpsimd if c % 2 == 0 else nc.vector
-            adder.tensor_tensor(out=noise_of[c][:], in0=noise_of[c][:], in1=bias_all[MU][:, cols], op=ADD)
+            nc.gpsimd.tensor_tensor(out=noise_of[c][:], in0=noise_of[c][:], in1=bias_all[MU][:, cols], op=ADD)
 
         def finish(c, mu_acc, first=0, width=N_CHUNK):
             m, h, cols = place(c)
@@ -225,7 +225,7 @@ def tile_vae_pb_kernel(
         for c in range(-LEAD, CHUNKS):
             begins = c + LEAD < CHUNKS
             prepares = FIRST_TILES <= c + TILE_LEAD < ROW_TILES
-            continues = 0 <= c + LEAD - 1 < CHUNKS
+            continues = 0 <= c + LEAD - NOISE_LAG < CHUNKS
             ends = c >= 0
 
             if begins:
@@ -237,11 +237,11 @@ def tile_vae_pb_kernel(
                 mu_accs = [mx_group(MU, c, first, width) for first, width in parts]
 
             if continues:
-                times_eps(c + LEAD - 1)
+                times_eps(c + LEAD - NOISE_LAG)
             if begins:
                 start_noise(c + LEAD, ls_acc)
             if continues:
-                plus_b_mu(c + LEAD - 1)
+                plus_b_mu(c + LEAD - NOISE_LAG)
             if prepares:
                 quantise(c + TILE_LEAD)
             if ends:

from contextlib import ExitStack

import concourse.mybir as mybir
from concourse.masks import make_identity

F32 = mybir.dt.float32
BF16 = mybir.dt.bfloat16
U8 = mybir.dt.uint8
U32 = mybir.dt.uint32
I32 = mybir.dt.int32
FP8X4 = mybir.dt.float8_e4m3fn_x4
ADD = mybir.AluOpType.add
MULT = mybir.AluOpType.mult
EXP = mybir.ActivationFunctionType.Exp

P = 128
PACK = 4
K_PASS = P * PACK
ROWS = 1024
K = 2048
N = 1024
N_CHUNK = 512
ROW_TILES = ROWS // P
PASSES = K // K_PASS
HALVES = N // N_CHUNK
CHUNKS = HALVES * ROW_TILES
QUADRANTS = 4
LEAD = 5
NOISE_LAG = 2
TILE_LEAD = LEAD + 3
FIRST_TILES = 4
MU = "mu"
LS = "ls"

FLOPS = 2 * ROWS * K * 2 * N


def tile_vae_pb_kernel(
    tc, hd, w_mu_words, w_mu_scales, b_mu, w_ls_words, w_ls_scales, b_ls, eps_x, out
):
    nc = tc.nc
    words_dram = {MU: w_mu_words, LS: w_ls_words}
    scales_dram = {MU: w_mu_scales, LS: w_ls_scales}
    bias_dram = {MU: b_mu, LS: b_ls}

    with ExitStack() as ctx:
        ctx.enter_context(tc.manual_schedule())
        keep = ctx.enter_context(tc.tile_pool(name="keep", bufs=1))
        stage = ctx.enter_context(tc.tile_pool(name="stage", bufs=FIRST_TILES))
        work = ctx.enter_context(tc.tile_pool(name="work", bufs=LEAD + 3))
        results = ctx.enter_context(tc.tile_pool(name="results", bufs=8))
        psum = ctx.enter_context(tc.psum_pool(name="psum", bufs=8))

        bias_in = {}
        for w in (LS, MU):
            bias_in[w] = keep.tile([1, N], BF16, name="bias_in_" + w)
            nc.sync.dma_start(out=bias_in[w][:], in_=bias_dram[w].unsqueeze(0))
        bias_rows = {}
        for w in (LS, MU):
            bias_rows[w] = keep.tile([P, N], BF16, name="bias_rows_" + w)
            nc.vector.memset(bias_rows[w][:], 0.0)
        ones = keep.tile([P, P], BF16)
        nc.vector.memset(ones[:], 1.0)
        ident = keep.tile([P, P], F32)
        make_identity(nc, ident[:])

        w_planes = {}
        for w in (LS, MU):
            w_planes[w] = keep.tile([P, N], U8, name="planes_" + w, align_bytes=64)
            nc.vector.memset(w_planes[w][:].bitcast(I32), 0)

        table_warmer = keep.tile([P, 1], F32)
        nc.vector.memset(table_warmer[:], 0.0)
        nc.scalar.activation(out=table_warmer[:], in_=table_warmer[:], func=EXP)

        for w in (LS, MU):
            nc.vector.tensor_copy(out=bias_rows[w][0:1, :], in_=bias_in[w][:])

        hd_sb = [keep.tile([P, K], BF16, name="hd%d" % m) for m in range(ROW_TILES)]
        eps_sb = [keep.tile([P, N], BF16, name="eps%d" % m) for m in range(ROW_TILES)]
        w_words = {}

        def load_hd(m):
            nc.sync.dma_start(out=hd_sb[m][:], in_=hd[m * P : (m + 1) * P, :])

        def load_eps(m):
            nc.sync.dma_start(out=eps_sb[m][:], in_=eps_x[m * P : (m + 1) * P, :])

        def load_scales(w):
            for quad in range(QUADRANTS):
                nc.sync.dma_start(
                    out=w_planes[w][32 * quad : 32 * quad + 16, :].bitcast(I32),
                    in_=scales_dram[w][:, 4 * quad : 4 * quad + 4, :].bitcast(I32),
                )

        def load_words(w, h):
            byte_cols = slice(h * N_CHUNK * PACK, (h + 1) * N_CHUNK * PACK)
            for first in range(0, PASSES, 2):
                pair = keep.tile([P, 2, N_CHUNK], U32, name="words_%s_%d_%d" % (w, h, first), align_bytes=64)
                nc.sync.dma_start(
                    out=pair[:].bitcast(I32),
                    in_=words_dram[w][first : first + 2]
                    .rearrange("g p n t -> p g (n t)")[:, :, byte_cols]
                    .bitcast(I32),
                )
                for j in range(2):
                    w_words[(w, h, first + j)] = pair[:, j, :]

        def load_weight_half(w, h):
            if h == 0:
                load_scales(w)
            load_words(w, h)

        for m in range(FIRST_TILES):
            load_hd(m)
        for c in range(-LEAD, CHUNKS):
            if c + LEAD < CHUNKS and (c + LEAD) % ROW_TILES == 0:
                load_weight_half(LS, (c + LEAD) // ROW_TILES)
            if FIRST_TILES <= c + TILE_LEAD < ROW_TILES:
                load_hd(c + TILE_LEAD)
            if 0 <= c + LEAD - NOISE_LAG < ROW_TILES:
                load_eps(c + LEAD - NOISE_LAG)
            if c >= 0 and c % ROW_TILES == 0:
                load_weight_half(MU, c // ROW_TILES)

        hd_codes = [
            keep.tile([P, PASSES * P], U32, name="hd_codes%d" % m, align_bytes=64)
            for m in range(ROW_TILES)
        ]
        hd_scales = [
            keep.tile([P, PASSES * P], U8, name="hd_scales%d" % m, align_bytes=64)
            for m in range(ROW_TILES)
        ]
        grouped_of = {}

        def transpose(m):
            pairs = hd_sb[m][:].bitcast(F32)
            grouped = stage.tile([P, PASSES, P, PACK], BF16, align_bytes=64)
            grouped_of[m] = grouped
            for first in range(0, PASSES, 2):
                flipped = psum.tile([P, 2, 2, P], F32, name="bank")
                for j in range(2):
                    g = first + j
                    for u in range(2):
                        nc.tensor.transpose(
                            flipped[:, j, u, :],
                            pairs[:, 256 * g + u : 256 * (g + 1) : 2],
                            ident[:],
                        )
                nc.scalar.copy(
                    out=grouped[:, first : first + 2, :, :].bitcast(F32),
                    in_=flipped[:].rearrange("p g u r -> p g r u"),
                )

        def quantise(m):
            nc.vector.quantize_mx(
                out=hd_codes[m][:].bitcast(FP8X4),
                scales=hd_scales[m][:],
                in_=grouped_of[m][:].rearrange("p g r t -> p (g r t)"),
            )

        bias_all = {}

        def broadcast_bias(w):
            bias_all[w] = keep.tile([P, N], F32, name="bias_all_" + w)
            for h in range(HALVES):
                cols = slice(h * N_CHUNK, (h + 1) * N_CHUNK)
                acc = psum.tile([P, N_CHUNK], F32, name="bank")
                nc.tensor.matmul(acc[:], lhsT=ones[:], rhs=bias_rows[w][:, cols], start=True, stop=True)
                nc.vector.tensor_copy(out=bias_all[w][:, cols], in_=acc[:])

        def place(c):
            h, m = divmod(c, ROW_TILES)
            return m, h, slice(h * N_CHUNK, (h + 1) * N_CHUNK)

        def mx_group(w, c, first=0, width=N_CHUNK):
            m, h, cols = place(c)
            acc = psum.tile([P, width], F32, name="bank")
            for g in range(PASSES):
                rows = slice(g * P, (g + 1) * P)
                nc.tensor.matmul_mx(
                    out=acc[:],
                    lhsT=hd_codes[m][:, rows].bitcast(FP8X4),
                    lhsT_scale=hd_scales[m][:, rows],
                    rhs=w_words[(w, h, g)][:, first : first + width].bitcast(FP8X4),
                    rhs_scale=w_planes[w][4 * g : P, cols.start + first : cols.start + first + width],
                    start=(g == 0),
                    stop=(g == PASSES - 1),
                )
            return acc

        noise_of = {}

        def start_noise(c, ls_acc):
            m, h, cols = place(c)
            noise_of[c] = work.tile([P, N_CHUNK], F32, name="noise")
            nc.vector.tensor_tensor(out=noise_of[c][:], in0=ls_acc[:], in1=bias_all[LS][:, cols], op=ADD)
            nc.scalar.activation(out=noise_of[c][:], in_=noise_of[c][:], func=EXP, scale=0.5)

        def times_eps(c):
            m, h, cols = place(c)
            nc.vector.tensor_tensor(out=noise_of[c][:], in0=noise_of[c][:], in1=eps_sb[m][:, cols], op=MULT)

        def plus_b_mu(c):
            m, h, cols = place(c)
            nc.gpsimd.tensor_tensor(out=noise_of[c][:], in0=noise_of[c][:], in1=bias_all[MU][:, cols], op=ADD)

        def finish(c, mu_acc, first=0, width=N_CHUNK):
            m, h, cols = place(c)
            result = results.tile([P, width], F32, name="result")
            nc.vector.tensor_tensor(
                out=result[:], in0=mu_acc[:], in1=noise_of[c][:, first : first + width], op=ADD
            )
            nc.sync.dma_start(
                out=out[m * P : (m + 1) * P, cols.start + first : cols.start + first + width], in_=result[:]
            )

        broadcast_bias(LS)
        broadcast_bias(MU)
        for m in range(FIRST_TILES):
            transpose(m)
        for m in range(FIRST_TILES):
            quantise(m)

        for c in range(-LEAD, CHUNKS):
            begins = c + LEAD < CHUNKS
            prepares = FIRST_TILES <= c + TILE_LEAD < ROW_TILES
            continues = 0 <= c + LEAD - NOISE_LAG < CHUNKS
            ends = c >= 0

            if begins:
                ls_acc = mx_group(LS, c + LEAD)
            if prepares:
                transpose(c + TILE_LEAD)
            parts = [(0, N_CHUNK)] if c < CHUNKS - 1 else [(0, N_CHUNK // 2), (N_CHUNK // 2, N_CHUNK // 2)]
            if ends:
                mu_accs = [mx_group(MU, c, first, width) for first, width in parts]

            if continues:
                times_eps(c + LEAD - NOISE_LAG)
            if begins:
                start_noise(c + LEAD, ls_acc)
            if continues:
                plus_b_mu(c + LEAD - NOISE_LAG)
            if prepares:
                quantise(c + TILE_LEAD)
            if ends:
                for mu_acc, (first, width) in zip(mu_accs, parts):
                    finish(c, mu_acc, first, width)
